import numpy as np
import ml_dtypes


def mxq(x, axis, fmt="e4m3"):
    dtype, down = {"e4m3": (ml_dtypes.float8_e4m3fn, 7), "e5m2": (ml_dtypes.float8_e5m2, 14)}[fmt]
    v = np.moveaxis(np.asarray(x, np.float32).astype(ml_dtypes.bfloat16).astype(np.float64), axis, -1)
    blocks = v.reshape(v.shape[:-1] + (-1, 32))
    amax = np.abs(blocks).max(-1, keepdims=True)
    byte = np.maximum(np.where(amax > 0, np.frexp(amax)[1] - 1 + 127, 0) - down, 1)
    scale = np.exp2(byte - 127.0)
    codes = (blocks / scale).astype(np.float32).astype(dtype).astype(np.float64)
    return np.moveaxis((codes * scale).reshape(v.shape), -1, axis)


WIDE = False


def mx_kscale(k):
    if not WIDE:
        return np.ones(k)
    levels = np.array([10, -10, 5, -5, 0])
    a = np.random.permutation(np.resize(levels, k // 512 * 4)).reshape(k // 512, 4)
    idx = np.arange(k)
    return np.exp2(a[idx // 512, idx % 128 // 32])


BF16 = ml_dtypes.bfloat16


def bf(x):
    return np.asarray(x, np.float32).astype(BF16)


def f64(x):
    return np.asarray(x).astype(np.float64)


E2M1 = np.array([0.0, 0.5, 1.0, 1.5, 2.0, 3.0, 4.0, 6.0, -0.0, -0.5, -1.0, -1.5, -2.0, -3.0, -4.0, -6.0])


def pack_weight(w, fmt):
    k, n = w.shape
    w = f64(bf(w)).reshape(k // 32, 32, n)
    amax = np.abs(w).max(1)
    if fmt == "e4m3":
        byte = np.frexp(amax)[1] - 1 + 127 - 7
    else:
        mant, ex = np.frexp(amax / 6.0)
        byte = np.where(mant > 0.5, ex, ex - 1) + 127
    byte = np.clip(np.where(amax > 0, byte, 1), 1, 254)
    scaled = (w * np.exp2(127.0 - byte)[:, None, :]).reshape(k, n).astype(np.float32)
    by_word = np.ascontiguousarray(scaled.reshape(k // 512, 128, 4, n).transpose(0, 1, 3, 2))
    if fmt == "e4m3":
        words = by_word.astype(ml_dtypes.float8_e4m3fn).view(np.uint8)
    else:
        c = by_word.astype(ml_dtypes.float4_e2m1fn).view(np.uint8) & 0xF
        words = c[..., 0::2] | (c[..., 1::2] << 4)
    return np.ascontiguousarray(words), np.ascontiguousarray(byte.astype(np.uint8).reshape(k // 512, 16, n))


def unpack_weight(words, scales, fmt):
    g, p, n, _ = words.shape
    if fmt == "e4m3":
        vals = np.ascontiguousarray(words).view(ml_dtypes.float8_e4m3fn).astype(np.float64)
    else:
        nib = np.empty((g, p, n, 4), np.uint8)
        nib[..., 0::2] = words & 0xF
        nib[..., 1::2] = words >> 4
        vals = E2M1[nib]
    vals = vals * np.repeat(np.exp2(scales.astype(np.float64) - 127.0), 8, axis=1)[..., None]
    return vals.transpose(0, 1, 3, 2).reshape(g * 512, n)


M, K, N = 1024, 1024, 4096


def setup_inputs():
    s = mx_kscale(K)
    W = np.random.standard_normal((K, N)) * 0.03 / s[:, None]
    w_words, w_scales = pack_weight(W, "e4m3")
    return {"x": bf(np.random.standard_normal((M, K)) * s), "w_words": w_words, "w_scales": w_scales,
            "bias": bf(np.random.standard_normal(N) * 0.3)}


def reference(x, w_words, w_scales, bias):
    W = unpack_weight(w_words, w_scales, "e4m3")
    return (mxq(f64(x), 1, "e4m3") @ W) + f64(bias)

@@ -1,0 +1,163 @@
+from contextlib import ExitStack
+
+import concourse.mybir as mybir
+from concourse.masks import make_identity
+
+F32 = mybir.dt.float32
+BF16 = mybir.dt.bfloat16
+I32 = mybir.dt.int32
+U32 = mybir.dt.uint32
+U8 = mybir.dt.uint8
+FP8X4 = mybir.dt.float8_e4m3fn_x4
+ADD = mybir.AluOpType.add
+
+P = 128
+M, K, N = 1024, 1024, 4096
+MT = M // P
+G = K // 512
+NW = 512
+NT = N // NW
+HALF = N // 2
+FLOPS = 2 * M * K * N
+
+
+def tile_fp4linear_kernel(tc, x, w_words, w_scales, bias, out):
+    nc = tc.nc
+    with ExitStack() as ctx:
+        keep = ctx.enter_context(tc.tile_pool(name="keep", bufs=1))
+        stage = ctx.enter_context(tc.tile_pool(name="stage", bufs=4))
+        outs = ctx.enter_context(tc.tile_pool(name="outs", bufs=10))
+        acc_pool = ctx.enter_context(tc.psum_pool(name="acc", bufs=6))
+        aux_pool = ctx.enter_context(tc.psum_pool(name="aux", bufs=2))
+
+        x_sb = keep.tile([P, MT, K], BF16)
+        xq = keep.tile([P, MT, G * P], U32, align_bytes=64)
+        xs = keep.tile([P, MT, G * P], U8, align_bytes=64)
+        w_sb = keep.tile([P, G, N], U32, align_bytes=64)
+        w_pl = keep.tile([P, N], U8, align_bytes=64)
+        bias_pad = keep.tile([P, N], BF16)
+        bias_bc = keep.tile([P, N], F32)
+        ident = keep.tile([P, P], F32)
+        ones = keep.tile([P, P], BF16)
+
+        x_v = x.rearrange("(p m) k -> p m k", m=MT)
+        out_v = out.rearrange("(p m) n -> p m n", m=MT)
+        w_v = w_words.rearrange("g p n t -> p g (n t)")
+
+        nc.vector.memset(w_pl[:].bitcast(I32), 0)
+        nc.vector.memset(bias_pad[:].bitcast(I32), 0)
+        nc.vector.memset(ones[:], 1.0)
+        make_identity(nc, ident[:])
+
+        def load_x(m0, m1):
+            nc.sync.dma_start(out=x_sb[:, m0:m1, :], in_=x_v[:, m0:m1, :])
+
+        def load_scales():
+            for g in range(G):
+                for q in range(4):
+                    row = 32 * q + 4 * g
+                    nc.sync.dma_start(
+                        out=w_pl[row : row + 4, :].bitcast(I32),
+                        in_=w_scales[g, 4 * q : 4 * q + 4, :].bitcast(I32),
+                    )
+
+        def load_w(c0, c1):
+            nc.sync.dma_start(
+                out=w_sb[:, :, c0:c1].bitcast(I32),
+                in_=w_v[:, :, 4 * c0 : 4 * c1].bitcast(I32),
+            )
+
+        load_x(0, 2)
+        load_scales()
+        nc.sync.dma_start(out=bias_pad[0:1, :], in_=bias.rearrange("(o n) -> o n", o=1))
+        load_w(0, 1024)
+        load_x(2, 4)
+        load_x(4, 8)
+        load_w(1024, 2048)
+        load_w(2048, 3072)
+        load_w(3072, 4096)
+
+        def prepare(mt):
+            xt = aux_pool.tile([P, G, 2, P], F32, tag="aux")
+            words = x_sb[:, mt, :].bitcast(F32)
+            for g in range(G):
+                for u in range(2):
+                    nc.tensor.transpose(
+                        xt[:, g, u, :],
+                        words[:, 256 * g + u : 256 * (g + 1) : 2],
+                        ident[:],
+                    )
+            xg = stage.tile([P, G * P * 4], BF16, align_bytes=64)
+            dst = xg[:].bitcast(F32).rearrange("p (g t u) -> p g t u", g=G, u=2)
+            src = xt[:].rearrange("p g u t -> p g t u")
+            if mt % 2 == 0:
+                nc.scalar.copy(out=dst, in_=src)
+            else:
+                nc.vector.tensor_copy(out=dst, in_=src)
+            return xg
+
+        def quantise(mt, xg):
+            nc.vector.quantize_mx(
+                out=xq[:, mt, :].bitcast(FP8X4), scales=xs[:, mt, :], in_=xg[:]
+            )
+
+        def spread_bias(nt):
+            cols = slice(nt * NW, (nt + 1) * NW)
+            pb = aux_pool.tile([P, NW], F32, tag="aux")
+            nc.tensor.matmul(
+                out=pb[:], lhsT=ones[:], rhs=bias_pad[:, cols], start=True, stop=True
+            )
+            nc.scalar.copy(out=bias_bc[:, cols], in_=pb[:])
+
+        def product(mt, nt, o_tile):
+            cols = slice(nt * NW, (nt + 1) * NW)
+            acc = acc_pool.tile([P, NW], F32)
+            for g in range(G):
+                nc.tensor.matmul_mx(
+                    out=acc[:],
+                    lhsT=xq[:, mt, g * P : (g + 1) * P].bitcast(FP8X4),
+                    lhsT_scale=xs[:, mt, g * P : (g + 1) * P],
+                    rhs=w_sb[:, g, cols].bitcast(FP8X4),
+                    rhs_scale=w_pl[4 * g : P, cols],
+                    start=(g == 0),
+                    stop=(g == G - 1),
+                )
+            lo = (nt * NW) % HALF
+            nc.vector.tensor_tensor(
+                out=o_tile[:, lo : lo + NW], in0=acc[:], in1=bias_bc[:, cols], op=ADD
+            )
+
+        def store(mt, h, o_tile):
+            nc.sync.dma_start(
+                out=out_v[:, mt, h * HALF : (h + 1) * HALF], in_=o_tile[:]
+            )
+
+        o_live = {}
+        for c in range(4):
+            for nt in (2 * c, 2 * c + 1):
+                spread_bias(nt)
+            for pair in ((0, 1), (2, 3)):
+                if c == 0:
+                    grouped = [prepare(mt) for mt in pair]
+                    for mt, xg in zip(pair, grouped):
+                        quantise(mt, xg)
+                for mt in pair:
+                    if c % 2 == 0:
+                        o_live[mt] = outs.tile([P, HALF], F32, name="o_tile", tag="o")
+                    for nt in (2 * c, 2 * c + 1):
+                        product(mt, nt, o_live[mt])
+            if c == 0:
+                for pair in ((4, 5), (6, 7)):
+                    grouped = [prepare(mt) for mt in pair]
+                    for mt, xg in zip(pair, grouped):
+                        quantise(mt, xg)
+            if c % 2 == 1:
+                for mt in range(4):
+                    store(mt, c // 2, o_live[mt])
+
+        for mt in range(4, MT):
+            for h in range(2):
+                o_tile = outs.tile([P, HALF], F32, name="o_tile", tag="o")
+                for nt in range(4 * h, 4 * h + 4):
+                    product(mt, nt, o_tile)
+                store(mt, h, o_tile)

@@ -18,48 +18,40 @@ G = K // 512
 NW = 512
 NT = N // NW
 HALF = N // 2
+UNIT = HALF // NW
 FLOPS = 2 * M * K * N
 
 
 def tile_fp4linear_kernel(tc, x, w_words, w_scales, bias, out):
     nc = tc.nc
     with ExitStack() as ctx:
+        ctx.enter_context(tc.manual_schedule())
         keep = ctx.enter_context(tc.tile_pool(name="keep", bufs=1))
         stage = ctx.enter_context(tc.tile_pool(name="stage", bufs=4))
-        outs = ctx.enter_context(tc.tile_pool(name="outs", bufs=10))
-        acc_pool = ctx.enter_context(tc.psum_pool(name="acc", bufs=6))
-        aux_pool = ctx.enter_context(tc.psum_pool(name="aux", bufs=2))
+        outs = ctx.enter_context(tc.tile_pool(name="outs", bufs=12))
+        banks = ctx.enter_context(tc.psum_pool(name="banks", bufs=8))
 
         x_sb = keep.tile([P, MT, K], BF16)
         xq = keep.tile([P, MT, G * P], U32, align_bytes=64)
         xs = keep.tile([P, MT, G * P], U8, align_bytes=64)
         w_sb = keep.tile([P, G, N], U32, align_bytes=64)
         w_pl = keep.tile([P, N], U8, align_bytes=64)
-        bias_pad = keep.tile([P, N], BF16)
+        bias8 = keep.tile([P, NW], BF16)
         bias_bc = keep.tile([P, N], F32)
         ident = keep.tile([P, P], F32)
-        ones = keep.tile([P, P], BF16)
+        sel = keep.tile([P, NT], BF16)
 
         x_v = x.rearrange("(p m) k -> p m k", m=MT)
         out_v = out.rearrange("(p m) n -> p m n", m=MT)
         w_v = w_words.rearrange("g p n t -> p g (n t)")
 
         nc.vector.memset(w_pl[:].bitcast(I32), 0)
-        nc.vector.memset(bias_pad[:].bitcast(I32), 0)
-        nc.vector.memset(ones[:], 1.0)
+        nc.vector.memset(bias8[:].bitcast(I32), 0)
         make_identity(nc, ident[:])
+        nc.vector.tensor_copy(out=sel[:], in_=ident[:, 0:NT])
 
         def load_x(m0, m1):
             nc.sync.dma_start(out=x_sb[:, m0:m1, :], in_=x_v[:, m0:m1, :])
-
-        def load_scales():
-            for g in range(G):
-                for q in range(4):
-                    row = 32 * q + 4 * g
-                    nc.sync.dma_start(
-                        out=w_pl[row : row + 4, :].bitcast(I32),
-                        in_=w_scales[g, 4 * q : 4 * q + 4, :].bitcast(I32),
-                    )
 
         def load_w(c0, c1):
             nc.sync.dma_start(
@@ -67,18 +59,25 @@ def tile_fp4linear_kernel(tc, x, w_words, w_scales, bias, out):
                 in_=w_v[:, :, 4 * c0 : 4 * c1].bitcast(I32),
             )
 
-        load_x(0, 2)
-        load_scales()
-        nc.sync.dma_start(out=bias_pad[0:1, :], in_=bias.rearrange("(o n) -> o n", o=1))
-        load_w(0, 1024)
-        load_x(2, 4)
-        load_x(4, 8)
+        load_x(0, 1)
+        load_x(1, 2)
+        load_w(0, 512)
+        load_w(512, 1024)
         load_w(1024, 2048)
-        load_w(2048, 3072)
-        load_w(3072, 4096)
+        load_x(2, 4)
+        nc.scalar.dma_start(
+            out=bias8[0:NT, :], in_=bias.rearrange("(j n) -> j n", j=NT)
+        )
+        load_x(4, 8)
+        load_w(2048, 4096)
+        for q in range(4):
+            nc.gpsimd.dma_start(
+                out=w_pl[32 * q : 32 * q + 8, :].bitcast(F32),
+                in_=w_scales[:, 4 * q : 4 * q + 4, :].bitcast(F32),
+            )
 
-        def prepare(mt):
-            xt = aux_pool.tile([P, G, 2, P], F32, tag="aux")
+        def transposes(mt):
+            xt = banks.tile([P, G, 2, P], F32, tag="bank", name="xt")
             words = x_sb[:, mt, :].bitcast(F32)
             for g in range(G):
                 for u in range(2):
@@ -87,13 +86,14 @@ def tile_fp4linear_kernel(tc, x, w_words, w_scales, bias, out):
                         words[:, 256 * g + u : 256 * (g + 1) : 2],
                         ident[:],
                     )
-            xg = stage.tile([P, G * P * 4], BF16, align_bytes=64)
-            dst = xg[:].bitcast(F32).rearrange("p (g t u) -> p g t u", g=G, u=2)
-            src = xt[:].rearrange("p g u t -> p g t u")
-            if mt % 2 == 0:
-                nc.scalar.copy(out=dst, in_=src)
-            else:
-                nc.vector.tensor_copy(out=dst, in_=src)
+            return xt
+
+        def regroup(xt):
+            xg = stage.tile([P, G * P * 4], BF16, align_bytes=64, name="xg")
+            nc.scalar.copy(
+                out=xg[:].bitcast(F32).rearrange("p (g t u) -> p g t u", g=G, u=2),
+                in_=xt[:].rearrange("p g u t -> p g t u"),
+            )
             return xg
 
         def quantise(mt, xg):
@@ -101,17 +101,30 @@ def tile_fp4linear_kernel(tc, x, w_words, w_scales, bias, out):
                 out=xq[:, mt, :].bitcast(FP8X4), scales=xs[:, mt, :], in_=xg[:]
             )
 
-        def spread_bias(nt):
-            cols = slice(nt * NW, (nt + 1) * NW)
-            pb = aux_pool.tile([P, NW], F32, tag="aux")
-            nc.tensor.matmul(
-                out=pb[:], lhsT=ones[:], rhs=bias_pad[:, cols], start=True, stop=True
-            )
-            nc.scalar.copy(out=bias_bc[:, cols], in_=pb[:])
+        def prepare(tiles):
+            planes = [transposes(mt) for mt in tiles]
+            grouped = [regroup(xt) for xt in planes]
+            for mt, xg in zip(tiles, grouped):
+                quantise(mt, xg)
 
-        def product(mt, nt, o_tile):
+        def spread_bias(j, on_vector):
+            cols = slice(j * NW, (j + 1) * NW)
+            pb = banks.tile([P, NW], F32, tag="bank", name="pb")
+            nc.tensor.matmul(
+                out=pb[:],
+                lhsT=sel[:, j : j + 1].to_broadcast([P, P]),
+                rhs=bias8[:],
+                start=True,
+                stop=True,
+            )
+            if on_vector:
+                nc.vector.tensor_copy(out=bias_bc[:, cols], in_=pb[:])
+            else:
+                nc.scalar.copy(out=bias_bc[:, cols], in_=pb[:])
+
+        def product(mt, nt, o_part, by_gpsimd):
             cols = slice(nt * NW, (nt + 1) * NW)
-            acc = acc_pool.tile([P, NW], F32)
+            acc = banks.tile([P, NW], F32, tag="bank", name="acc")
             for g in range(G):
                 nc.tensor.matmul_mx(
                     out=acc[:],
@@ -122,42 +135,43 @@ def tile_fp4linear_kernel(tc, x, w_words, w_scales, bias, out):
                     start=(g == 0),
                     stop=(g == G - 1),
                 )
-            lo = (nt * NW) % HALF
-            nc.vector.tensor_tensor(
-                out=o_tile[:, lo : lo + NW], in0=acc[:], in1=bias_bc[:, cols], op=ADD
-            )
+            if by_gpsimd:
+                nc.scalar.copy(out=o_part, in_=acc[:])
+                nc.gpsimd.tensor_tensor(
+                    out=o_part, in0=o_part, in1=bias_bc[:, cols], op=ADD
+                )
+            else:
+                nc.vector.tensor_tensor(
+                    out=o_part, in0=acc[:], in1=bias_bc[:, cols], op=ADD
+                )
 
-        def store(mt, h, o_tile):
-            nc.sync.dma_start(
-                out=out_v[:, mt, h * HALF : (h + 1) * HALF], in_=o_tile[:]
-            )
+        def unit(mt, h, gp_pos, cuts):
+            o_tile = outs.tile([P, HALF], F32, tag="o", name="o_tile")
+            done = 0
+            for pos in range(UNIT):
+                product(
+                    mt,
+                    UNIT * h + pos,
+                    o_tile[:, pos * NW : (pos + 1) * NW],
+                    pos == gp_pos,
+                )
+                if pos + 1 in cuts:
+                    a, b = done * NW, (pos + 1) * NW
+                    nc.sync.dma_start(
+                        out=out_v[:, mt, h * HALF + a : h * HALF + b],
+                        in_=o_tile[:, a:b],
+                    )
+                    done = pos + 1
 
-        o_live = {}
-        for c in range(4):
-            for nt in (2 * c, 2 * c + 1):
-                spread_bias(nt)
-            for pair in ((0, 1), (2, 3)):
-                if c == 0:
-                    grouped = [prepare(mt) for mt in pair]
-                    for mt, xg in zip(pair, grouped):
-                        quantise(mt, xg)
-                for mt in pair:
-                    if c % 2 == 0:
-                        o_live[mt] = outs.tile([P, HALF], F32, name="o_tile", tag="o")
-                    for nt in (2 * c, 2 * c + 1):
-                        product(mt, nt, o_live[mt])
-            if c == 0:
-                for pair in ((4, 5), (6, 7)):
-                    grouped = [prepare(mt) for mt in pair]
-                    for mt, xg in zip(pair, grouped):
-                        quantise(mt, xg)
-            if c % 2 == 1:
-                for mt in range(4):
-                    store(mt, c // 2, o_live[mt])
-
-        for mt in range(4, MT):
-            for h in range(2):
-                o_tile = outs.tile([P, HALF], F32, name="o_tile", tag="o")
-                for nt in range(4 * h, 4 * h + 4):
-                    product(mt, nt, o_tile)
-                store(mt, h, o_tile)
+        prepare((0, 1))
+        for j in range(4):
+            spread_bias(j, on_vector=(j % 2 == 1))
+        for mt in range(MT):
+            unit(mt, 0, 1, (UNIT,))
+            if mt in (0, 2, 4):
+                prepare((mt + 2, mt + 3))
+            if mt >= 3 and mt + 1 < NT:
+                spread_bias(mt + 1, on_vector=False)
+        for mt in range(MT - 1):
+            unit(mt, 1, 1, (UNIT,))
+        unit(MT - 1, 1, 0, (2, 3, 4))

@@ -45,8 +45,8 @@ def tile_fp4linear_kernel(tc, x, w_words, w_scales, bias, out):
         out_v = out.rearrange("(p m) n -> p m n", m=MT)
         w_v = w_words.rearrange("g p n t -> p g (n t)")
 
-        nc.vector.memset(w_pl[:].bitcast(I32), 0)
         nc.vector.memset(bias8[:].bitcast(I32), 0)
+        nc.vector.memset(w_pl[:].bitcast(I32), 0)
         make_identity(nc, ident[:])
         nc.vector.tensor_copy(out=sel[:], in_=ident[:, 0:NT])
 
@@ -60,15 +60,13 @@ def tile_fp4linear_kernel(tc, x, w_words, w_scales, bias, out):
             )
 
         load_x(0, 1)
+        nc.sync.dma_start(out=bias8[0:NT, :], in_=bias.rearrange("(j n) -> j n", j=NT))
         load_x(1, 2)
+        load_x(2, 4)
+        load_x(4, 8)
         load_w(0, 512)
         load_w(512, 1024)
         load_w(1024, 2048)
-        load_x(2, 4)
-        nc.scalar.dma_start(
-            out=bias8[0:NT, :], in_=bias.rearrange("(j n) -> j n", j=NT)
-        )
-        load_x(4, 8)
         load_w(2048, 4096)
         for q in range(4):
             nc.gpsimd.dma_start(
@@ -76,17 +74,14 @@ def tile_fp4linear_kernel(tc, x, w_words, w_scales, bias, out):
                 in_=w_scales[:, 4 * q : 4 * q + 4, :].bitcast(F32),
             )
 
-        def transposes(mt):
-            xt = banks.tile([P, G, 2, P], F32, tag="bank", name="xt")
+        def transposes(mt, xt, g):
             words = x_sb[:, mt, :].bitcast(F32)
-            for g in range(G):
-                for u in range(2):
-                    nc.tensor.transpose(
-                        xt[:, g, u, :],
-                        words[:, 256 * g + u : 256 * (g + 1) : 2],
-                        ident[:],
-                    )
-            return xt
+            for u in range(2):
+                nc.tensor.transpose(
+                    xt[:, g, u, :],
+                    words[:, 256 * g + u : 256 * (g + 1) : 2],
+                    ident[:],
+                )
 
         def regroup(xt):
             xg = stage.tile([P, G * P * 4], BF16, align_bytes=64, name="xg")
@@ -101,14 +96,7 @@ def tile_fp4linear_kernel(tc, x, w_words, w_scales, bias, out):
                 out=xq[:, mt, :].bitcast(FP8X4), scales=xs[:, mt, :], in_=xg[:]
             )
 
-        def prepare(tiles):
-            planes = [transposes(mt) for mt in tiles]
-            grouped = [regroup(xt) for xt in planes]
-            for mt, xg in zip(tiles, grouped):
-                quantise(mt, xg)
-
-        def spread_bias(j, on_vector):
-            cols = slice(j * NW, (j + 1) * NW)
+        def spread_bias(j):
             pb = banks.tile([P, NW], F32, tag="bank", name="pb")
             nc.tensor.matmul(
                 out=pb[:],
@@ -117,7 +105,11 @@ def tile_fp4linear_kernel(tc, x, w_words, w_scales, bias, out):
                 start=True,
                 stop=True,
             )
-            if on_vector:
+            return pb
+
+        def keep_bias(j, pb):
+            cols = slice(j * NW, (j + 1) * NW)
+            if j % 2 == 0:
                 nc.vector.tensor_copy(out=bias_bc[:, cols], in_=pb[:])
             else:
                 nc.scalar.copy(out=bias_bc[:, cols], in_=pb[:])
@@ -145,7 +137,7 @@ def tile_fp4linear_kernel(tc, x, w_words, w_scales, bias, out):
                     out=o_part, in0=acc[:], in1=bias_bc[:, cols], op=ADD
                 )
 
-        def unit(mt, h, gp_pos, cuts):
+        def unit(mt, h, gp_set, cuts):
             o_tile = outs.tile([P, HALF], F32, tag="o", name="o_tile")
             done = 0
             for pos in range(UNIT):
@@ -153,7 +145,7 @@ def tile_fp4linear_kernel(tc, x, w_words, w_scales, bias, out):
                     mt,
                     UNIT * h + pos,
                     o_tile[:, pos * NW : (pos + 1) * NW],
-                    pos == gp_pos,
+                    pos in gp_set,
                 )
                 if pos + 1 in cuts:
                     a, b = done * NW, (pos + 1) * NW
@@ -163,15 +155,21 @@ def tile_fp4linear_kernel(tc, x, w_words, w_scales, bias, out):
                     )
                     done = pos + 1
 
-        prepare((0, 1))
-        for j in range(4):
-            spread_bias(j, on_vector=(j % 2 == 1))
         for mt in range(MT):
-            unit(mt, 0, 1, (UNIT,))
-            if mt in (0, 2, 4):
-                prepare((mt + 2, mt + 3))
-            if mt >= 3 and mt + 1 < NT:
-                spread_bias(mt + 1, on_vector=False)
-        for mt in range(MT - 1):
-            unit(mt, 1, 1, (UNIT,))
-        unit(MT - 1, 1, 0, (2, 3, 4))
+            xt = banks.tile([P, G, 2, P], F32, tag="bank", name="xt")
+            spread = []
+            for g in range(G):
+                j = G * (mt - 1) + g
+                if 0 <= j < NT:
+                    spread.append((j, spread_bias(j)))
+                transposes(mt, xt, g)
+            xg = regroup(xt)
+            for j, pb in spread:
+                keep_bias(j, pb)
+            quantise(mt, xg)
+
+        units = [(mt, h) for h in range(2) for mt in range(MT)]
+        for i, (mt, h) in enumerate(units[:-1]):
+            gp_set = [pos for pos in range(UNIT) if (UNIT * i + pos) % 3 == 1]
+            unit(mt, h, gp_set, (UNIT,))
+        unit(MT - 1, 1, (0,), (2, 3, 4))

@@ -59,20 +59,24 @@ def tile_fp4linear_kernel(tc, x, w_words, w_scales, bias, out):
                 in_=w_v[:, :, 4 * c0 : 4 * c1].bitcast(I32),
             )
 
+        def load_scales(g, q):
+            row = 32 * q + 4 * g
+            nc.sync.dma_start(
+                out=w_pl[row : row + 4, :].bitcast(I32),
+                in_=w_scales[g, 4 * q : 4 * q + 4, :].bitcast(I32),
+            )
+
         load_x(0, 1)
         nc.sync.dma_start(out=bias8[0:NT, :], in_=bias.rearrange("(j n) -> j n", j=NT))
-        load_x(1, 2)
-        load_x(2, 4)
+        load_x(1, 4)
         load_x(4, 8)
-        load_w(0, 512)
-        load_w(512, 1024)
+        for q in range(4):
+            load_scales(0, q)
+        load_w(0, 1024)
+        for q in range(4):
+            load_scales(1, q)
         load_w(1024, 2048)
         load_w(2048, 4096)
-        for q in range(4):
-            nc.gpsimd.dma_start(
-                out=w_pl[32 * q : 32 * q + 8, :].bitcast(F32),
-                in_=w_scales[:, 4 * q : 4 * q + 4, :].bitcast(F32),
-            )
 
         def transposes(mt, xt, g):
             words = x_sb[:, mt, :].bitcast(F32)

@@ -19,6 +19,7 @@ NW = 512
 NT = N // NW
 HALF = N // 2
 UNIT = HALF // NW
+PAD = 48
 FLOPS = 2 * M * K * N
 
 
@@ -32,10 +33,10 @@ def tile_fp4linear_kernel(tc, x, w_words, w_scales, bias, out):
         banks = ctx.enter_context(tc.psum_pool(name="banks", bufs=8))
 
         x_sb = keep.tile([P, MT, K], BF16)
-        xq = keep.tile([P, MT, G * P], U32, align_bytes=64)
-        xs = keep.tile([P, MT, G * P], U8, align_bytes=64)
-        w_sb = keep.tile([P, G, N], U32, align_bytes=64)
-        w_pl = keep.tile([P, N], U8, align_bytes=64)
+        xq = keep.tile([P, PAD + MT * G * P], U32, align_bytes=256)
+        xs = keep.tile([P, MT * G, 2 * P], U8, align_bytes=256)
+        w_sb = keep.tile([P, G, N], U32, align_bytes=256)
+        w_pl = keep.tile([P, N], U8, align_bytes=256)
         bias8 = keep.tile([P, NW], BF16)
         bias_bc = keep.tile([P, N], F32)
         ident = keep.tile([P, P], F32)
@@ -59,24 +60,20 @@ def tile_fp4linear_kernel(tc, x, w_words, w_scales, bias, out):
                 in_=w_v[:, :, 4 * c0 : 4 * c1].bitcast(I32),
             )
 
-        def load_scales(g, q):
-            row = 32 * q + 4 * g
-            nc.sync.dma_start(
-                out=w_pl[row : row + 4, :].bitcast(I32),
-                in_=w_scales[g, 4 * q : 4 * q + 4, :].bitcast(I32),
-            )
-
         load_x(0, 1)
         nc.sync.dma_start(out=bias8[0:NT, :], in_=bias.rearrange("(j n) -> j n", j=NT))
-        load_x(1, 4)
+        load_x(1, 2)
+        load_x(2, 4)
         load_x(4, 8)
-        for q in range(4):
-            load_scales(0, q)
-        load_w(0, 1024)
-        for q in range(4):
-            load_scales(1, q)
+        load_w(0, 512)
+        load_w(512, 1024)
         load_w(1024, 2048)
         load_w(2048, 4096)
+        for q in range(4):
+            nc.gpsimd.dma_start(
+                out=w_pl[32 * q : 32 * q + 8, :].bitcast(F32),
+                in_=w_scales[:, 4 * q : 4 * q + 4, :].bitcast(F32),
+            )
 
         def transposes(mt, xt, g):
             words = x_sb[:, mt, :].bitcast(F32)
@@ -96,9 +93,13 @@ def tile_fp4linear_kernel(tc, x, w_words, w_scales, bias, out):
             return xg
 
         def quantise(mt, xg):
-            nc.vector.quantize_mx(
-                out=xq[:, mt, :].bitcast(FP8X4), scales=xs[:, mt, :], in_=xg[:]
-            )
+            for g in range(G):
+                i = mt * G + g
+                nc.vector.quantize_mx(
+                    out=xq[:, PAD + i * P : PAD + (i + 1) * P].bitcast(FP8X4),
+                    scales=xs[:, i, 0:P],
+                    in_=xg[:, g * 4 * P : (g + 1) * 4 * P],
+                )
 
         def spread_bias(j):
             pb = banks.tile([P, NW], F32, tag="bank", name="pb")
@@ -122,10 +123,11 @@ def tile_fp4linear_kernel(tc, x, w_words, w_scales, bias, out):
             cols = slice(nt * NW, (nt + 1) * NW)
             acc = banks.tile([P, NW], F32, tag="bank", name="acc")
             for g in range(G):
+                i = mt * G + g
                 nc.tensor.matmul_mx(
                     out=acc[:],
-                    lhsT=xq[:, mt, g * P : (g + 1) * P].bitcast(FP8X4),
-                    lhsT_scale=xs[:, mt, g * P : (g + 1) * P],
+                    lhsT=xq[:, PAD + i * P : PAD + (i + 1) * P].bitcast(FP8X4),
+                    lhsT_scale=xs[:, i, 0:P],
                     rhs=w_sb[:, g, cols].bitcast(FP8X4),
                     rhs_scale=w_pl[4 * g : P, cols],
                     start=(g == 0),

@@ -19,7 +19,6 @@ NW = 512
 NT = N // NW
 HALF = N // 2
 UNIT = HALF // NW
-PAD = 48
 FLOPS = 2 * M * K * N
 
 
@@ -33,19 +32,21 @@ def tile_fp4linear_kernel(tc, x, w_words, w_scales, bias, out):
         banks = ctx.enter_context(tc.psum_pool(name="banks", bufs=8))
 
         x_sb = keep.tile([P, MT, K], BF16)
-        xq = keep.tile([P, PAD + MT * G * P], U32, align_bytes=256)
-        xs = keep.tile([P, MT * G, 2 * P], U8, align_bytes=256)
-        w_sb = keep.tile([P, G, N], U32, align_bytes=256)
-        w_pl = keep.tile([P, N], U8, align_bytes=256)
+        xq = keep.tile([P, MT, G * P], U32, align_bytes=64)
+        xs = keep.tile([P, MT, G * P], U8, align_bytes=64)
+        w_sb = keep.tile([P, G, N], U32, align_bytes=64)
+        w_pl = keep.tile([P, N], U8, align_bytes=64)
         bias8 = keep.tile([P, NW], BF16)
         bias_bc = keep.tile([P, N], F32)
         ident = keep.tile([P, P], F32)
         sel = keep.tile([P, NT], BF16)
+        warm = keep.tile([P, NW], BF16)
 
         x_v = x.rearrange("(p m) k -> p m k", m=MT)
         out_v = out.rearrange("(p m) n -> p m n", m=MT)
         w_v = w_words.rearrange("g p n t -> p g (n t)")
 
+        nc.vector.memset(warm[:].bitcast(I32), 0)
         nc.vector.memset(bias8[:].bitcast(I32), 0)
         nc.vector.memset(w_pl[:].bitcast(I32), 0)
         make_identity(nc, ident[:])
@@ -93,13 +94,9 @@ def tile_fp4linear_kernel(tc, x, w_words, w_scales, bias, out):
             return xg
 
         def quantise(mt, xg):
-            for g in range(G):
-                i = mt * G + g
-                nc.vector.quantize_mx(
-                    out=xq[:, PAD + i * P : PAD + (i + 1) * P].bitcast(FP8X4),
-                    scales=xs[:, i, 0:P],
-                    in_=xg[:, g * 4 * P : (g + 1) * 4 * P],
-                )
+            nc.vector.quantize_mx(
+                out=xq[:, mt, :].bitcast(FP8X4), scales=xs[:, mt, :], in_=xg[:]
+            )
 
         def spread_bias(j):
             pb = banks.tile([P, NW], F32, tag="bank", name="pb")
@@ -123,11 +120,10 @@ def tile_fp4linear_kernel(tc, x, w_words, w_scales, bias, out):
             cols = slice(nt * NW, (nt + 1) * NW)
             acc = banks.tile([P, NW], F32, tag="bank", name="acc")
             for g in range(G):
-                i = mt * G + g
                 nc.tensor.matmul_mx(
                     out=acc[:],
-                    lhsT=xq[:, PAD + i * P : PAD + (i + 1) * P].bitcast(FP8X4),
-                    lhsT_scale=xs[:, i, 0:P],
+                    lhsT=xq[:, mt, g * P : (g + 1) * P].bitcast(FP8X4),
+                    lhsT_scale=xs[:, mt, g * P : (g + 1) * P],
                     rhs=w_sb[:, g, cols].bitcast(FP8X4),
                     rhs_scale=w_pl[4 * g : P, cols],
                     start=(g == 0),
@@ -143,9 +139,8 @@ def tile_fp4linear_kernel(tc, x, w_words, w_scales, bias, out):
                     out=o_part, in0=acc[:], in1=bias_bc[:, cols], op=ADD
                 )
 
-        def unit(mt, h, gp_set, cuts):
+        def unit(mt, h, gp_set, stores):
             o_tile = outs.tile([P, HALF], F32, tag="o", name="o_tile")
-            done = 0
             for pos in range(UNIT):
                 product(
                     mt,
@@ -153,13 +148,18 @@ def tile_fp4linear_kernel(tc, x, w_words, w_scales, bias, out):
                     o_tile[:, pos * NW : (pos + 1) * NW],
                     pos in gp_set,
                 )
-                if pos + 1 in cuts:
-                    a, b = done * NW, (pos + 1) * NW
+                for first, last in stores.get(pos, ()):
+                    a, b = first * NW, last * NW
                     nc.sync.dma_start(
                         out=out_v[:, mt, h * HALF + a : h * HALF + b],
                         in_=o_tile[:, a:b],
                     )
-                    done = pos + 1
+
+        wp = banks.tile([P, NW], F32, tag="bank", name="wp")
+        for i in range(4):
+            nc.tensor.matmul(
+                out=wp[:], lhsT=warm[:, 0:P], rhs=warm[:], start=True, stop=True
+            )
 
         for mt in range(MT):
             xt = banks.tile([P, G, 2, P], F32, tag="bank", name="xt")
@@ -175,7 +175,9 @@ def tile_fp4linear_kernel(tc, x, w_words, w_scales, bias, out):
             quantise(mt, xg)
 
         units = [(mt, h) for h in range(2) for mt in range(MT)]
+        whole = {3: [(0, 4)]}
+        halves = {1: [(0, 2)], 3: [(2, 4)]}
         for i, (mt, h) in enumerate(units[:-1]):
             gp_set = [pos for pos in range(UNIT) if (UNIT * i + pos) % 3 == 1]
-            unit(mt, h, gp_set, (UNIT,))
-        unit(MT - 1, 1, (0,), (2, 3, 4))
+            unit(mt, h, gp_set, whole if i < len(units) - 3 else halves)
+        unit(MT - 1, 1, (0,), {1: [(1, 2)], 2: [(2, 3), (0, 1)], 3: [(3, 4)]})

@@ -61,15 +61,17 @@ def tile_fp4linear_kernel(tc, x, w_words, w_scales, bias, out):
                 in_=w_v[:, :, 4 * c0 : 4 * c1].bitcast(I32),
             )
 
+        def held_back_loads(chunks):
+            first = chunks[0][0]
+            nc.vector.memset(w_sb[:, 0, first : first + 1].bitcast(I32), 0)
+            for c0, c1 in chunks:
+                load_w(c0, c1)
+
         load_x(0, 1)
         nc.sync.dma_start(out=bias8[0:NT, :], in_=bias.rearrange("(j n) -> j n", j=NT))
         load_x(1, 2)
         load_x(2, 4)
         load_x(4, 8)
-        load_w(0, 512)
-        load_w(512, 1024)
-        load_w(1024, 2048)
-        load_w(2048, 4096)
         for q in range(4):
             nc.gpsimd.dma_start(
                 out=w_pl[32 * q : 32 * q + 8, :].bitcast(F32),
@@ -172,6 +174,10 @@ def tile_fp4linear_kernel(tc, x, w_words, w_scales, bias, out):
             xg = regroup(xt)
             for j, pb in spread:
                 keep_bias(j, pb)
+            if mt == 1:
+                held_back_loads(((0, 512), (512, 1024)))
+            if mt == 3:
+                held_back_loads(((1024, 2048), (2048, 4096)))
             quantise(mt, xg)
 
         units = [(mt, h) for h in range(2) for mt in range(MT)]

from contextlib import ExitStack

import concourse.mybir as mybir
from concourse.masks import make_identity

F32 = mybir.dt.float32
BF16 = mybir.dt.bfloat16
I32 = mybir.dt.int32
U32 = mybir.dt.uint32
U8 = mybir.dt.uint8
FP8X4 = mybir.dt.float8_e4m3fn_x4
ADD = mybir.AluOpType.add

P = 128
M, K, N = 1024, 1024, 4096
MT = M // P
G = K // 512
NW = 512
NT = N // NW
HALF = N // 2
UNIT = HALF // NW
FLOPS = 2 * M * K * N


def tile_fp4linear_kernel(tc, x, w_words, w_scales, bias, out):
    nc = tc.nc
    with ExitStack() as ctx:
        ctx.enter_context(tc.manual_schedule())
        keep = ctx.enter_context(tc.tile_pool(name="keep", bufs=1))
        stage = ctx.enter_context(tc.tile_pool(name="stage", bufs=4))
        outs = ctx.enter_context(tc.tile_pool(name="outs", bufs=12))
        banks = ctx.enter_context(tc.psum_pool(name="banks", bufs=8))

        x_sb = keep.tile([P, MT, K], BF16)
        xq = keep.tile([P, MT, G * P], U32, align_bytes=64)
        xs = keep.tile([P, MT, G * P], U8, align_bytes=64)
        w_sb = keep.tile([P, G, N], U32, align_bytes=64)
        w_pl = keep.tile([P, N], U8, align_bytes=64)
        bias8 = keep.tile([P, NW], BF16)
        bias_bc = keep.tile([P, N], F32)
        ident = keep.tile([P, P], F32)
        sel = keep.tile([P, NT], BF16)
        warm = keep.tile([P, NW], BF16)

        x_v = x.rearrange("(p m) k -> p m k", m=MT)
        out_v = out.rearrange("(p m) n -> p m n", m=MT)
        w_v = w_words.rearrange("g p n t -> p g (n t)")

        nc.vector.memset(warm[:].bitcast(I32), 0)
        nc.vector.memset(bias8[:].bitcast(I32), 0)
        nc.vector.memset(w_pl[:].bitcast(I32), 0)
        make_identity(nc, ident[:])
        nc.vector.tensor_copy(out=sel[:], in_=ident[:, 0:NT])

        def load_x(m0, m1):
            nc.sync.dma_start(out=x_sb[:, m0:m1, :], in_=x_v[:, m0:m1, :])

        def load_w(c0, c1):
            nc.sync.dma_start(
                out=w_sb[:, :, c0:c1].bitcast(I32),
                in_=w_v[:, :, 4 * c0 : 4 * c1].bitcast(I32),
            )

        def held_back_loads(chunks):
            first = chunks[0][0]
            nc.vector.memset(w_sb[:, 0, first : first + 1].bitcast(I32), 0)
            for c0, c1 in chunks:
                load_w(c0, c1)

        load_x(0, 1)
        nc.sync.dma_start(out=bias8[0:NT, :], in_=bias.rearrange("(j n) -> j n", j=NT))
        load_x(1, 2)
        load_x(2, 4)
        load_x(4, 8)
        for q in range(4):
            nc.gpsimd.dma_start(
                out=w_pl[32 * q : 32 * q + 8, :].bitcast(F32),
                in_=w_scales[:, 4 * q : 4 * q + 4, :].bitcast(F32),
            )

        def transposes(mt, xt, g):
            words = x_sb[:, mt, :].bitcast(F32)
            for u in range(2):
                nc.tensor.transpose(
                    xt[:, g, u, :],
                    words[:, 256 * g + u : 256 * (g + 1) : 2],
                    ident[:],
                )

        def regroup(xt):
            xg = stage.tile([P, G * P * 4], BF16, align_bytes=64, name="xg")
            nc.scalar.copy(
                out=xg[:].bitcast(F32).rearrange("p (g t u) -> p g t u", g=G, u=2),
                in_=xt[:].rearrange("p g u t -> p g t u"),
            )
            return xg

        def quantise(mt, xg):
            nc.vector.quantize_mx(
                out=xq[:, mt, :].bitcast(FP8X4), scales=xs[:, mt, :], in_=xg[:]
            )

        def spread_bias(j):
            pb = banks.tile([P, NW], F32, tag="bank", name="pb")
            nc.tensor.matmul(
                out=pb[:],
                lhsT=sel[:, j : j + 1].to_broadcast([P, P]),
                rhs=bias8[:],
                start=True,
                stop=True,
            )
            return pb

        def keep_bias(j, pb):
            cols = slice(j * NW, (j + 1) * NW)
            if j % 2 == 0:
                nc.vector.tensor_copy(out=bias_bc[:, cols], in_=pb[:])
            else:
                nc.scalar.copy(out=bias_bc[:, cols], in_=pb[:])

        def product(mt, nt, o_part, by_gpsimd):
            cols = slice(nt * NW, (nt + 1) * NW)
            acc = banks.tile([P, NW], F32, tag="bank", name="acc")
            for g in range(G):
                nc.tensor.matmul_mx(
                    out=acc[:],
                    lhsT=xq[:, mt, g * P : (g + 1) * P].bitcast(FP8X4),
                    lhsT_scale=xs[:, mt, g * P : (g + 1) * P],
                    rhs=w_sb[:, g, cols].bitcast(FP8X4),
                    rhs_scale=w_pl[4 * g : P, cols],
                    start=(g == 0),
                    stop=(g == G - 1),
                )
            if by_gpsimd:
                nc.scalar.copy(out=o_part, in_=acc[:])
                nc.gpsimd.tensor_tensor(
                    out=o_part, in0=o_part, in1=bias_bc[:, cols], op=ADD
                )
            else:
                nc.vector.tensor_tensor(
                    out=o_part, in0=acc[:], in1=bias_bc[:, cols], op=ADD
                )

        def unit(mt, h, gp_set, stores):
            o_tile = outs.tile([P, HALF], F32, tag="o", name="o_tile")
            for pos in range(UNIT):
                product(
                    mt,
                    UNIT * h + pos,
                    o_tile[:, pos * NW : (pos + 1) * NW],
                    pos in gp_set,
                )
                for first, last in stores.get(pos, ()):
                    a, b = first * NW, last * NW
                    nc.sync.dma_start(
                        out=out_v[:, mt, h * HALF + a : h * HALF + b],
                        in_=o_tile[:, a:b],
                    )

        wp = banks.tile([P, NW], F32, tag="bank", name="wp")
        for i in range(4):
            nc.tensor.matmul(
                out=wp[:], lhsT=warm[:, 0:P], rhs=warm[:], start=True, stop=True
            )

        for mt in range(MT):
            xt = banks.tile([P, G, 2, P], F32, tag="bank", name="xt")
            spread = []
            for g in range(G):
                j = G * (mt - 1) + g
                if 0 <= j < NT:
                    spread.append((j, spread_bias(j)))
                transposes(mt, xt, g)
            xg = regroup(xt)
            for j, pb in spread:
                keep_bias(j, pb)
            if mt == 1:
                held_back_loads(((0, 512), (512, 1024)))
            if mt == 3:
                held_back_loads(((1024, 2048), (2048, 4096)))
            quantise(mt, xg)

        units = [(mt, h) for h in range(2) for mt in range(MT)]
        whole = {3: [(0, 4)]}
        halves = {1: [(0, 2)], 3: [(2, 4)]}
        for i, (mt, h) in enumerate(units[:-1]):
            gp_set = [pos for pos in range(UNIT) if (UNIT * i + pos) % 3 == 1]
            unit(mt, h, gp_set, whole if i < len(units) - 3 else halves)
        unit(MT - 1, 1, (0,), {1: [(1, 2)], 2: [(2, 3), (0, 1)], 3: [(3, 4)]})
